import numpy as np
import ml_dtypes


def mxq(x, axis, fmt="e4m3"):
    dtype, down = {"e4m3": (ml_dtypes.float8_e4m3fn, 7), "e5m2": (ml_dtypes.float8_e5m2, 14)}[fmt]
    v = np.moveaxis(np.asarray(x, np.float32).astype(ml_dtypes.bfloat16).astype(np.float64), axis, -1)
    blocks = v.reshape(v.shape[:-1] + (-1, 32))
    amax = np.abs(blocks).max(-1, keepdims=True)
    byte = np.maximum(np.where(amax > 0, np.frexp(amax)[1] - 1 + 127, 0) - down, 1)
    scale = np.exp2(byte - 127.0)
    codes = (blocks / scale).astype(np.float32).astype(dtype).astype(np.float64)
    return np.moveaxis((codes * scale).reshape(v.shape), -1, axis)


WIDE = False


def mx_kscale(k):
    if not WIDE:
        return np.ones(k)
    levels = np.array([10, -10, 5, -5, 0])
    if k % 512:
        return np.exp2(np.random.permutation(np.resize(levels, k // 32))).repeat(32)
    a = np.empty((k // 512, 16))
    for p in range(k // 512):
        a[p, :8] = np.random.permutation(np.resize(levels, 8))
        for g in range(8):
            far = levels[np.abs(levels - a[p, g]) >= 10]
            a[p, g + 8] = far[np.random.randint(len(far))]
    return np.exp2(a.ravel()).repeat(32)


BF16 = ml_dtypes.bfloat16


def bf(x):
    return np.asarray(x, np.float32).astype(BF16)


def f64(x):
    return np.asarray(x).astype(np.float64)


B, S, K, N = 4, 2048, 1024, 128
FP8_MAX = 448.0
EPS = 1e-12


def setup_inputs():
    s = mx_kscale(K)
    return {"x": bf(np.random.standard_normal((B, S, K)) * s),
            "weight": bf(np.random.standard_normal((K, N)) * 1.28 / np.sqrt(K) / s[:, None])}


def reference(x, weight):
    x = f64(x)
    weight = f64(weight)
    b, sl, k = x.shape
    n = weight.shape[1]
    x2 = x.reshape(-1, k)
    x_scale = FP8_MAX / np.maximum(np.max(np.abs(x2)), EPS)
    w_scale = FP8_MAX / np.maximum(np.max(np.abs(weight)), EPS)
    x_sim = np.clip(x2 * x_scale, -FP8_MAX, FP8_MAX)
    w_sim = np.clip(weight * w_scale, -FP8_MAX, FP8_MAX)
    out = (mxq(x_sim, 1, "e4m3") @ mxq(w_sim, 0, "e4m3")) * (1.0 / (x_scale * w_scale))
    return out.reshape(b, sl, n)

@@ -1,0 +1,310 @@
+from contextlib import ExitStack
+
+import concourse.mybir as mybir
+from concourse.masks import make_identity
+
+F32 = mybir.dt.float32
+BF16 = mybir.dt.bfloat16
+I32 = mybir.dt.int32
+U32 = mybir.dt.uint32
+U8 = mybir.dt.uint8
+FP8X4 = mybir.dt.float8_e4m3fn_x4
+ALU = mybir.AluOpType
+ACT = mybir.ActivationFunctionType
+AX = mybir.AxisListType
+
+P = 128
+ROWS = 8192
+K = 1024
+N_OUT = 128
+ROW_TILES = ROWS // P
+TILES_PER_CHUNK = 4
+CHUNKS = ROW_TILES // TILES_PER_CHUNK
+CHUNK_COLS = TILES_PER_CHUNK * K
+FLOW_TILES = TILES_PER_CHUNK - 1
+FLOW_COLS = FLOW_TILES * K
+PASSES = K // 512
+WORDS = K // 2
+ABS_MASK = 0x7FFF7FFF
+FP8_MAX = 448.0
+EPS = 1e-12
+EXTRA_ABS_COLS = 192
+LATE_EXTRA_ABS_COLS = 1280
+EXTRA_SCALE_COLS = 192
+HELD_AHEAD = 3
+DEFERRED = 3
+
+FLOPS = 2 * ROWS * K * N_OUT
+
+
+def tile_modelnew_t_kernel(tc, x, weight, out):
+    nc = tc.nc
+    x_flat = x.flatten_outer_dims().rearrange("(p t) k -> p (t k)", t=ROW_TILES)
+    out_flat = out.flatten_outer_dims().rearrange("(p t) n -> p (t n)", t=ROW_TILES)
+
+    with ExitStack() as stack:
+        keep = stack.enter_context(tc.tile_pool(name="keep", bufs=1))
+        natural_pool = stack.enter_context(tc.tile_pool(name="natural", bufs=4))
+        tree_pool = stack.enter_context(tc.tile_pool(name="tree", bufs=2))
+        mx_pool = stack.enter_context(tc.tile_pool(name="mx", bufs=3))
+        result_pool = stack.enter_context(tc.tile_pool(name="result", bufs=3))
+        banks = stack.enter_context(tc.psum_pool(name="banks", bufs=8))
+        stack.enter_context(tc.manual_schedule())
+
+        identity = keep.tile([P, P], F32)
+        make_identity(nc, identity[:])
+        over_448 = keep.tile([P, P], F32)
+        nc.vector.memset(over_448[:], 1.0 / FP8_MAX)
+        running = keep.tile([P, K], BF16)
+        nc.vector.memset(running[:], 0.0)
+
+        def spread(column, name):
+            repeated = keep.tile([P, P], F32, name=name + "_repeated")
+            nc.vector.tensor_scalar(
+                out=repeated[:], in0=over_448[:], scalar1=column[:, 0:1], scalar2=EPS / FP8_MAX, op0=ALU.mult, op1=ALU.max
+            )
+            turned = banks.tile([P, P], F32, name=name + "_turned", tag="bank")
+            nc.tensor.transpose(turned[:], repeated[:], identity[:])
+            return turned
+
+        def inverse_scale_of(turned, name):
+            inverse_scale = keep.tile([P, 1], F32, name=name + "_inverse_scale")
+            nc.vector.reduce_max(out=inverse_scale[:], in_=turned[:], axis=AX.X)
+            return inverse_scale
+
+        def reciprocal_of(inverse_scale, name):
+            the_scale = keep.tile([P, 1], F32, name=name + "_scale")
+            nc.vector.reciprocal(out=the_scale[:], in_=inverse_scale[:])
+            return the_scale
+
+        def clear_signs(out_cols, in_cols):
+            nc.vector.tensor_scalar(
+                out=out_cols.bitcast(I32), in0=in_cols.bitcast(I32), scalar1=ABS_MASK, scalar2=None, op0=ALU.bitwise_and
+            )
+
+        def transpose_tile(words):
+            flipped = banks.tile([P, WORDS], F32, name="flipped", tag="bank")
+            for g in range(PASSES):
+                for u in range(2):
+                    a = 2 * g + u
+                    nc.tensor.transpose(
+                        flipped[:, a * P : (a + 1) * P], words[:, 256 * g + u : 256 * (g + 1) : 2], identity[:]
+                    )
+            return flipped
+
+        w_raw = keep.tile([P, PASSES, 4 * N_OUT], BF16)
+        w_flat = w_raw[:].rearrange("p g c -> p (g c)")
+        w_abs = keep.tile([P, K], BF16)
+        w_half = keep.tile([P, K // 2], BF16)
+        w_column = keep.tile([P, 1], F32)
+        w_grouped = keep.tile([P, PASSES, N_OUT, 4], BF16, align_bytes=64)
+        w_codes = keep.tile([P, PASSES * N_OUT], U32, align_bytes=64)
+        w_scales = keep.tile([P, PASSES * N_OUT], U8, align_bytes=64)
+
+        def weight_group(g, w_scale):
+            nc.vector.tensor_scalar(
+                out=w_grouped[:, g],
+                in0=w_raw[:, g, :].rearrange("p (j n) -> p n j", j=4),
+                scalar1=w_scale[:, 0:1],
+                scalar2=None,
+                op0=ALU.mult,
+            )
+
+        grouped = []
+        naturals = {}
+        magnitudes = {}
+        halves = {}
+        quarters = {}
+        flow_banks = {}
+        held_banks = {}
+
+        def load_and_transpose(s):
+            chunk = keep.tile([P, CHUNK_COLS], BF16, name="grouped%d" % s, align_bytes=64)
+            grouped.append(chunk)
+            natural = natural_pool.tile([P, FLOW_COLS], BF16, name="natural")
+            naturals[s] = natural
+            first = s * CHUNK_COLS
+            queue = nc.sync
+            queue.dma_start(out=chunk[:, :K], in_=x_flat[:, first : first + K])
+            pieces = FLOW_TILES if s == 0 else 1
+            width = FLOW_COLS // pieces
+            for i in range(pieces):
+                queue.dma_start(
+                    out=natural[:, i * width : (i + 1) * width],
+                    in_=x_flat[:, first + K + i * width : first + K + (i + 1) * width],
+                )
+            words = natural[:].bitcast(F32)
+            for t in range(FLOW_TILES):
+                flow_banks[(s, t)] = transpose_tile(words[:, t * WORDS : (t + 1) * WORDS])
+
+        def copy_out(s):
+            chunk_words = grouped[s][:].bitcast(F32).rearrange(
+                "p (t g r u) -> p t g r u", t=TILES_PER_CHUNK, g=PASSES, r=P, u=2
+            )
+            for t in range(FLOW_TILES):
+                nc.scalar.copy(
+                    out=chunk_words[:, t + 1],
+                    in_=flow_banks[(s, t)][:].rearrange("p (g u r) -> p g r u", g=PASSES, u=2, r=P),
+                )
+
+        def magnitude_of(s):
+            natural = naturals[s]
+            magnitude = tree_pool.tile([P, CHUNK_COLS], BF16, name="magnitude")
+            magnitudes[s] = magnitude
+            extra = LATE_EXTRA_ABS_COLS if s > CHUNKS - DEFERRED else EXTRA_ABS_COLS
+            nc.scalar.activation(out=magnitude[:, :K], in_=grouped[s][:, :K], func=ACT.Abs)
+            nc.scalar.activation(out=magnitude[:, K : K + extra], in_=natural[:, :extra], func=ACT.Abs)
+            clear_signs(magnitude[:, K + extra :], natural[:, extra:])
+
+        def fold_half(s):
+            magnitude = magnitudes[s]
+            half = tree_pool.tile([P, CHUNK_COLS // 2], BF16, name="half")
+            halves[s] = half
+            nc.vector.tensor_tensor(
+                out=half[:], in0=magnitude[:, : CHUNK_COLS // 2], in1=magnitude[:, CHUNK_COLS // 2 :], op=ALU.max
+            )
+
+        def fold_quarter(s):
+            half = halves[s]
+            quarter = tree_pool.tile([P, K], BF16, name="quarter")
+            quarters[s] = quarter
+            nc.vector.tensor_tensor(out=quarter[:], in0=half[:, :K], in1=half[:, K:], op=ALU.max)
+
+        def fold_running(values):
+            nc.vector.tensor_tensor(out=running[:], in0=running[:], in1=values, op=ALU.max)
+
+        load_and_transpose(0)
+        nc.sync.dma_start(out=w_raw[:], in_=weight.rearrange("(g p j) n -> p g (j n)", g=PASSES, p=P, j=4))
+        first_magnitude = tree_pool.tile([P, CHUNK_COLS], BF16, name="magnitude")
+
+        def first_mask(i):
+            source = grouped[0][:, :K] if i == 0 else naturals[0][:, (i - 1) * K : i * K]
+            clear_signs(first_magnitude[:, i * K : (i + 1) * K], source)
+
+        def first_fold(i):
+            fold_running(first_magnitude[:, i * K : (i + 1) * K])
+
+        first_mask(0)
+        first_mask(1)
+        first_fold(0)
+        first_mask(2)
+        first_fold(1)
+        first_mask(3)
+        first_fold(2)
+        nc.scalar.activation(out=w_abs[:], in_=w_flat, func=ACT.Abs)
+        first_fold(3)
+        nc.vector.tensor_tensor(out=w_half[:], in0=w_abs[:, : K // 2], in1=w_abs[:, K // 2 :], op=ALU.max)
+        nc.vector.reduce_max(out=w_column[:], in_=w_half[:], axis=AX.X)
+        w_turned = spread(w_column, "w")
+        w_facts = {}
+        for s in range(1, CHUNKS):
+            load_and_transpose(s)
+            if s >= 2:
+                fold_half(s - 1)
+            magnitude_of(s)
+            if s - 1 < CHUNKS - DEFERRED:
+                copy_out(s - 1)
+            if s == 1:
+                w_facts["inverse_scale"] = inverse_scale_of(w_turned, "w")
+            if s >= 2:
+                fold_quarter(s - 1)
+            if s == 2:
+                w_facts["scale"] = reciprocal_of(w_facts["inverse_scale"], "w")
+            if s >= 3:
+                fold_running(quarters[s - 2][:])
+        for s in range(CHUNKS - DEFERRED, CHUNKS):
+            copy_out(s)
+
+        def transpose_held(c):
+            held_banks[c] = transpose_tile(grouped[c][:, :K].bitcast(F32))
+
+        for c in range(HELD_AHEAD):
+            transpose_held(c)
+        fold_half(CHUNKS - 1)
+        fold_running(quarters[CHUNKS - 2][:])
+        fold_quarter(CHUNKS - 1)
+        fold_running(quarters[CHUNKS - 1][:])
+        x_column = keep.tile([P, 1], F32)
+        nc.vector.reduce_max(out=x_column[:], in_=running[:], axis=AX.X)
+        x_turned = spread(x_column, "x")
+        weight_group(0, w_facts["scale"])
+        weight_group(1, w_facts["scale"])
+        x_inverse_scale = inverse_scale_of(x_turned, "x")
+        nc.vector.quantize_mx(
+            out=w_codes[:].bitcast(FP8X4), scales=w_scales[:], in_=w_grouped[:].rearrange("p g n j -> p (g n j)")
+        )
+        x_scale = reciprocal_of(x_inverse_scale, "x")
+        final_factor = keep.tile([P, 1], F32)
+        nc.vector.tensor_tensor(out=final_factor[:], in0=x_inverse_scale[:], in1=w_facts["inverse_scale"][:], op=ALU.mult)
+
+        def scale(c):
+            flat = grouped[c]
+            pairs = held_banks[c][:].bitcast(BF16)
+            for g in range(PASSES):
+                cols = slice(g * 512, (g + 1) * 512)
+                nc.scalar.activation(
+                    out=flat[:, cols].rearrange("p (r u e) -> p r u e", r=P, u=2, e=2),
+                    in_=pairs[:, cols].rearrange("p (u r e) -> p r u e", u=2, r=P, e=2),
+                    func=ACT.Copy,
+                    scale=x_scale[:, 0:1],
+                )
+            split = K + EXTRA_SCALE_COLS
+            nc.scalar.activation(out=flat[:, K:split], in_=flat[:, K:split], func=ACT.Copy, scale=x_scale[:, 0:1])
+            nc.vector.tensor_scalar(
+                out=flat[:, split:], in0=flat[:, split:], scalar1=x_scale[:, 0:1], scalar2=None, op0=ALU.mult
+            )
+
+        def multiply(c, first_tile, tiles):
+            width = tiles * K
+            codes = mx_pool.tile([P, width // 4], U32, name="codes", align_bytes=64)
+            scales = mx_pool.tile([P, width // 4], U8, name="scales", align_bytes=64)
+            nc.vector.quantize_mx(
+                out=codes[:].bitcast(FP8X4), scales=scales[:], in_=grouped[c][:, first_tile * K : first_tile * K + width]
+            )
+            acc = banks.tile([P, tiles, N_OUT], F32, name="acc", tag="bank")
+            for t in range(tiles):
+                for g in range(PASSES):
+                    x_cols = slice((t * PASSES + g) * P, (t * PASSES + g + 1) * P)
+                    w_cols = slice(g * N_OUT, (g + 1) * N_OUT)
+                    nc.tensor.matmul_mx(
+                        out=acc[:, t, :],
+                        lhsT=codes[:, x_cols].bitcast(FP8X4),
+                        lhsT_scale=scales[:, x_cols],
+                        rhs=w_codes[:, w_cols].bitcast(FP8X4),
+                        rhs_scale=w_scales[:, w_cols],
+                        start=(g == 0),
+                        stop=(g == PASSES - 1),
+                    )
+            return acc
+
+        def finish(c, first_tile, tiles, acc):
+            width = tiles * N_OUT
+            if tiles == TILES_PER_CHUNK:
+                result = result_pool.tile([P, width], F32, name="result")
+            else:
+                result = keep.tile([P, width], F32, name="piece%d" % first_tile)
+            nc.scalar.activation(
+                out=result[:], in_=acc[:].rearrange("p t n -> p (t n)"), func=ACT.Copy, scale=final_factor[:, 0:1]
+            )
+            first_col = (c * TILES_PER_CHUNK + first_tile) * N_OUT
+            nc.sync.dma_start(out=out_flat[:, first_col : first_col + width], in_=result[:])
+
+        scale(0)
+        scale(1)
+        products = {}
+        for c in range(CHUNKS - 1):
+            products[c] = multiply(c, 0, TILES_PER_CHUNK)
+            if c + HELD_AHEAD < CHUNKS:
+                transpose_held(c + HELD_AHEAD)
+            if c + 2 < CHUNKS:
+                scale(c + 2)
+            if c >= 1:
+                finish(c - 1, 0, TILES_PER_CHUNK, products[c - 1])
+        last = CHUNKS - 1
+        for t in range(TILES_PER_CHUNK):
+            products[(last, t)] = multiply(last, t, 1)
+            if t == 0:
+                finish(last - 1, 0, TILES_PER_CHUNK, products[last - 1])
+            else:
+                finish(last, t - 1, 1, products[(last, t - 1)])
+        finish(last, TILES_PER_CHUNK - 1, 1, products[(last, TILES_PER_CHUNK - 1)])

@@ -45,7 +45,7 @@ def tile_modelnew_t_kernel(tc, x, weight, out):
     with ExitStack() as stack:
         keep = stack.enter_context(tc.tile_pool(name="keep", bufs=1))
         natural_pool = stack.enter_context(tc.tile_pool(name="natural", bufs=4))
-        tree_pool = stack.enter_context(tc.tile_pool(name="tree", bufs=2))
+        tree_pool = stack.enter_context(tc.tile_pool(name="tree", bufs=3))
         mx_pool = stack.enter_context(tc.tile_pool(name="mx", bufs=3))
         result_pool = stack.enter_context(tc.tile_pool(name="result", bufs=3))
         banks = stack.enter_context(tc.psum_pool(name="banks", bufs=8))
@@ -53,18 +53,22 @@ def tile_modelnew_t_kernel(tc, x, weight, out):
 
         identity = keep.tile([P, P], F32)
         make_identity(nc, identity[:])
-        over_448 = keep.tile([P, P], F32)
-        nc.vector.memset(over_448[:], 1.0 / FP8_MAX)
-        running = keep.tile([P, K], BF16)
-        nc.vector.memset(running[:], 0.0)
+        maxima = keep.tile([P, TILES_PER_CHUNK + CHUNKS - 1], F32)
 
-        def spread(column, name):
-            repeated = keep.tile([P, P], F32, name=name + "_repeated")
+        def spread(columns, name):
+            column = keep.tile([P, 1], F32, name=name + "_column")
+            unused = keep.tile(columns.shape, F32, name=name + "_unused")
             nc.vector.tensor_scalar(
-                out=repeated[:], in0=over_448[:], scalar1=column[:, 0:1], scalar2=EPS / FP8_MAX, op0=ALU.mult, op1=ALU.max
+                out=unused[:],
+                in0=columns,
+                scalar1=1.0 / FP8_MAX,
+                scalar2=EPS / FP8_MAX,
+                op0=ALU.mult,
+                op1=ALU.max,
+                accum_out=column[:],
             )
             turned = banks.tile([P, P], F32, name=name + "_turned", tag="bank")
-            nc.tensor.transpose(turned[:], repeated[:], identity[:])
+            nc.tensor.transpose(turned[:], column[:, 0:1].to_broadcast([P, P]), identity[:])
             return turned
 
         def inverse_scale_of(turned, name):
@@ -95,8 +99,7 @@ def tile_modelnew_t_kernel(tc, x, weight, out):
         w_raw = keep.tile([P, PASSES, 4 * N_OUT], BF16)
         w_flat = w_raw[:].rearrange("p g c -> p (g c)")
         w_abs = keep.tile([P, K], BF16)
-        w_half = keep.tile([P, K // 2], BF16)
-        w_column = keep.tile([P, 1], F32)
+        w_maximum = keep.tile([P, 1], F32)
         w_grouped = keep.tile([P, PASSES, N_OUT, 4], BF16, align_bytes=64)
         w_codes = keep.tile([P, PASSES * N_OUT], U32, align_bytes=64)
         w_scales = keep.tile([P, PASSES * N_OUT], U8, align_bytes=64)
@@ -113,8 +116,6 @@ def tile_modelnew_t_kernel(tc, x, weight, out):
         grouped = []
         naturals = {}
         magnitudes = {}
-        halves = {}
-        quarters = {}
         flow_banks = {}
         held_banks = {}
 
@@ -156,22 +157,16 @@ def tile_modelnew_t_kernel(tc, x, weight, out):
             nc.scalar.activation(out=magnitude[:, K : K + extra], in_=natural[:, :extra], func=ACT.Abs)
             clear_signs(magnitude[:, K + extra :], natural[:, extra:])
 
-        def fold_half(s):
-            magnitude = magnitudes[s]
-            half = tree_pool.tile([P, CHUNK_COLS // 2], BF16, name="half")
-            halves[s] = half
-            nc.vector.tensor_tensor(
-                out=half[:], in0=magnitude[:, : CHUNK_COLS // 2], in1=magnitude[:, CHUNK_COLS // 2 :], op=ALU.max
+        def maximum_of(values, column):
+            unused = tree_pool.tile([P, CHUNK_COLS], BF16, name="unused")
+            width = values.shape[1]
+            nc.vector.tensor_scalar(
+                out=unused[:, :width], in0=values, scalar1=0.0, scalar2=0.0, op0=ALU.max, op1=ALU.max, accum_out=column
             )
 
-        def fold_quarter(s):
-            half = halves[s]
-            quarter = tree_pool.tile([P, K], BF16, name="quarter")
-            quarters[s] = quarter
-            nc.vector.tensor_tensor(out=quarter[:], in0=half[:, :K], in1=half[:, K:], op=ALU.max)
-
-        def fold_running(values):
-            nc.vector.tensor_tensor(out=running[:], in0=running[:], in1=values, op=ALU.max)
+        def chunk_maximum(s):
+            piece = TILES_PER_CHUNK - 1 + s
+            maximum_of(magnitudes[s][:], maxima[:, piece : piece + 1])
 
         load_and_transpose(0)
         nc.sync.dma_start(out=w_raw[:], in_=weight.rearrange("(g p j) n -> p g (j n)", g=PASSES, p=P, j=4))
@@ -182,7 +177,7 @@ def tile_modelnew_t_kernel(tc, x, weight, out):
             clear_signs(first_magnitude[:, i * K : (i + 1) * K], source)
 
         def first_fold(i):
-            fold_running(first_magnitude[:, i * K : (i + 1) * K])
+            maximum_of(first_magnitude[:, i * K : (i + 1) * K], maxima[:, i : i + 1])
 
         first_mask(0)
         first_mask(1)
@@ -193,25 +188,20 @@ def tile_modelnew_t_kernel(tc, x, weight, out):
         first_fold(2)
         nc.scalar.activation(out=w_abs[:], in_=w_flat, func=ACT.Abs)
         first_fold(3)
-        nc.vector.tensor_tensor(out=w_half[:], in0=w_abs[:, : K // 2], in1=w_abs[:, K // 2 :], op=ALU.max)
-        nc.vector.reduce_max(out=w_column[:], in_=w_half[:], axis=AX.X)
-        w_turned = spread(w_column, "w")
+        maximum_of(w_abs[:], w_maximum[:])
+        w_turned = spread(w_maximum[:], "w")
         w_facts = {}
         for s in range(1, CHUNKS):
             load_and_transpose(s)
-            if s >= 2:
-                fold_half(s - 1)
             magnitude_of(s)
             if s - 1 < CHUNKS - DEFERRED:
                 copy_out(s - 1)
             if s == 1:
                 w_facts["inverse_scale"] = inverse_scale_of(w_turned, "w")
             if s >= 2:
-                fold_quarter(s - 1)
+                chunk_maximum(s - 1)
             if s == 2:
                 w_facts["scale"] = reciprocal_of(w_facts["inverse_scale"], "w")
-            if s >= 3:
-                fold_running(quarters[s - 2][:])
         for s in range(CHUNKS - DEFERRED, CHUNKS):
             copy_out(s)
 
@@ -220,13 +210,8 @@ def tile_modelnew_t_kernel(tc, x, weight, out):
 
         for c in range(HELD_AHEAD):
             transpose_held(c)
-        fold_half(CHUNKS - 1)
-        fold_running(quarters[CHUNKS - 2][:])
-        fold_quarter(CHUNKS - 1)
-        fold_running(quarters[CHUNKS - 1][:])
-        x_column = keep.tile([P, 1], F32)
-        nc.vector.reduce_max(out=x_column[:], in_=running[:], axis=AX.X)
-        x_turned = spread(x_column, "x")
+        chunk_maximum(CHUNKS - 1)
+        x_turned = spread(maxima[:], "x")
         weight_group(0, w_facts["scale"])
         weight_group(1, w_facts["scale"])
         x_inverse_scale = inverse_scale_of(x_turned, "x")

@@ -28,10 +28,10 @@ WORDS = K // 2
 ABS_MASK = 0x7FFF7FFF
 FP8_MAX = 448.0
 EPS = 1e-12
-EXTRA_ABS_COLS = 192
+EXTRA_ABS_COLS = 64
 LATE_EXTRA_ABS_COLS = 1280
-EXTRA_SCALE_COLS = 192
-HELD_AHEAD = 3
+EXTRA_SCALE_COLS = 320
+HELD_AHEAD = 5
 DEFERRED = 3
 
 FLOPS = 2 * ROWS * K * N_OUT
@@ -105,12 +105,13 @@ def tile_modelnew_t_kernel(tc, x, weight, out):
         w_scales = keep.tile([P, PASSES * N_OUT], U8, align_bytes=64)
 
         def weight_group(g, w_scale):
-            nc.vector.tensor_scalar(
+            nc.gpsimd.tensor_scalar(
                 out=w_grouped[:, g],
                 in0=w_raw[:, g, :].rearrange("p (j n) -> p n j", j=4),
                 scalar1=w_scale[:, 0:1],
-                scalar2=None,
+                scalar2=1.0,
                 op0=ALU.mult,
+                op1=ALU.mult,
             )
 
         grouped = []
@@ -169,39 +170,48 @@ def tile_modelnew_t_kernel(tc, x, weight, out):
             maximum_of(magnitudes[s][:], maxima[:, piece : piece + 1])
 
         load_and_transpose(0)
-        nc.sync.dma_start(out=w_raw[:], in_=weight.rearrange("(g p j) n -> p g (j n)", g=PASSES, p=P, j=4))
         first_magnitude = tree_pool.tile([P, CHUNK_COLS], BF16, name="magnitude")
+        first_sources = [grouped[0][:, :K]] + [naturals[0][:, i * K : (i + 1) * K] for i in range(FLOW_TILES)]
 
         def first_mask(i):
-            source = grouped[0][:, :K] if i == 0 else naturals[0][:, (i - 1) * K : i * K]
-            clear_signs(first_magnitude[:, i * K : (i + 1) * K], source)
+            clear_signs(first_magnitude[:, i * K : (i + 1) * K], first_sources[i])
 
-        def first_fold(i):
+        def first_maximum(i):
             maximum_of(first_magnitude[:, i * K : (i + 1) * K], maxima[:, i : i + 1])
 
+        nc.scalar.activation(out=first_magnitude[:, K : 2 * K], in_=first_sources[1], func=ACT.Abs)
         first_mask(0)
-        first_mask(1)
-        first_fold(0)
+        first_maximum(0)
         first_mask(2)
-        first_fold(1)
+        first_maximum(1)
         first_mask(3)
-        first_fold(2)
-        nc.scalar.activation(out=w_abs[:], in_=w_flat, func=ACT.Abs)
-        first_fold(3)
-        maximum_of(w_abs[:], w_maximum[:])
-        w_turned = spread(w_maximum[:], "w")
+        first_maximum(2)
+        first_maximum(3)
+
         w_facts = {}
         for s in range(1, CHUNKS):
             load_and_transpose(s)
+            if s == 3:
+                nc.sync.dma_start(out=w_raw[:], in_=weight.rearrange("(g p j) n -> p g (j n)", g=PASSES, p=P, j=4))
+            if s == 2:
+                chunk_maximum(1)
             magnitude_of(s)
             if s - 1 < CHUNKS - DEFERRED:
                 copy_out(s - 1)
-            if s == 1:
-                w_facts["inverse_scale"] = inverse_scale_of(w_turned, "w")
-            if s >= 2:
+            if s >= 3:
                 chunk_maximum(s - 1)
-            if s == 2:
+            if s == 5:
+                nc.scalar.activation(out=w_abs[:], in_=w_flat, func=ACT.Abs)
+            if s == 6:
+                maximum_of(w_abs[:], w_maximum[:])
+            if s == 7:
+                w_facts["turned"] = spread(w_maximum[:], "w")
+            if s == 8:
+                w_facts["inverse_scale"] = inverse_scale_of(w_facts["turned"], "w")
+            if s == 9:
                 w_facts["scale"] = reciprocal_of(w_facts["inverse_scale"], "w")
+                weight_group(0, w_facts["scale"])
+                weight_group(1, w_facts["scale"])
         for s in range(CHUNKS - DEFERRED, CHUNKS):
             copy_out(s)
 
@@ -212,15 +222,13 @@ def tile_modelnew_t_kernel(tc, x, weight, out):
             transpose_held(c)
         chunk_maximum(CHUNKS - 1)
         x_turned = spread(maxima[:], "x")
-        weight_group(0, w_facts["scale"])
-        weight_group(1, w_facts["scale"])
-        x_inverse_scale = inverse_scale_of(x_turned, "x")
         nc.vector.quantize_mx(
             out=w_codes[:].bitcast(FP8X4), scales=w_scales[:], in_=w_grouped[:].rearrange("p g n j -> p (g n j)")
         )
+        x_inverse_scale = inverse_scale_of(x_turned, "x")
         x_scale = reciprocal_of(x_inverse_scale, "x")
         final_factor = keep.tile([P, 1], F32)
-        nc.vector.tensor_tensor(out=final_factor[:], in0=x_inverse_scale[:], in1=w_facts["inverse_scale"][:], op=ALU.mult)
+        nc.gpsimd.tensor_tensor(out=final_factor[:], in0=x_inverse_scale[:], in1=w_facts["inverse_scale"][:], op=ALU.mult)
 
         def scale(c):
             flat = grouped[c]

@@ -31,7 +31,7 @@ EPS = 1e-12
 EXTRA_ABS_COLS = 64
 LATE_EXTRA_ABS_COLS = 1280
 EXTRA_SCALE_COLS = 320
-HELD_AHEAD = 5
+HELD_AHEAD = 3
 DEFERRED = 3
 
 FLOPS = 2 * ROWS * K * N_OUT
@@ -55,7 +55,7 @@ def tile_modelnew_t_kernel(tc, x, weight, out):
         make_identity(nc, identity[:])
         maxima = keep.tile([P, TILES_PER_CHUNK + CHUNKS - 1], F32)
 
-        def spread(columns, name):
+        def column_of(columns, name):
             column = keep.tile([P, 1], F32, name=name + "_column")
             unused = keep.tile(columns.shape, F32, name=name + "_unused")
             nc.vector.tensor_scalar(
@@ -67,6 +67,9 @@ def tile_modelnew_t_kernel(tc, x, weight, out):
                 op1=ALU.max,
                 accum_out=column[:],
             )
+            return column
+
+        def turn(column, name):
             turned = banks.tile([P, P], F32, name=name + "_turned", tag="bank")
             nc.tensor.transpose(turned[:], column[:, 0:1].to_broadcast([P, P]), identity[:])
             return turned
@@ -205,10 +208,12 @@ def tile_modelnew_t_kernel(tc, x, weight, out):
             if s == 6:
                 maximum_of(w_abs[:], w_maximum[:])
             if s == 7:
-                w_facts["turned"] = spread(w_maximum[:], "w")
-            if s == 8:
+                w_facts["column"] = column_of(w_maximum[:], "w")
+            if s == 10:
+                w_facts["turned"] = turn(w_facts["column"], "w")
+            if s == 11:
                 w_facts["inverse_scale"] = inverse_scale_of(w_facts["turned"], "w")
-            if s == 9:
+            if s == 12:
                 w_facts["scale"] = reciprocal_of(w_facts["inverse_scale"], "w")
                 weight_group(0, w_facts["scale"])
                 weight_group(1, w_facts["scale"])
@@ -218,10 +223,11 @@ def tile_modelnew_t_kernel(tc, x, weight, out):
         def transpose_held(c):
             held_banks[c] = transpose_tile(grouped[c][:, :K].bitcast(F32))
 
-        for c in range(HELD_AHEAD):
-            transpose_held(c)
+        transpose_held(0)
         chunk_maximum(CHUNKS - 1)
-        x_turned = spread(maxima[:], "x")
+        x_turned = turn(column_of(maxima[:], "x"), "x")
+        for c in range(1, HELD_AHEAD):
+            transpose_held(c)
         nc.vector.quantize_mx(
             out=w_codes[:].bitcast(FP8X4), scales=w_scales[:], in_=w_grouped[:].rearrange("p g n j -> p (g n j)")
         )
@@ -286,9 +292,9 @@ def tile_modelnew_t_kernel(tc, x, weight, out):
         scale(1)
         products = {}
         for c in range(CHUNKS - 1):
-            products[c] = multiply(c, 0, TILES_PER_CHUNK)
             if c + HELD_AHEAD < CHUNKS:
                 transpose_held(c + HELD_AHEAD)
+            products[c] = multiply(c, 0, TILES_PER_CHUNK)
             if c + 2 < CHUNKS:
                 scale(c + 2)
             if c >= 1:

@@ -30,7 +30,7 @@ FP8_MAX = 448.0
 EPS = 1e-12
 EXTRA_ABS_COLS = 64
 LATE_EXTRA_ABS_COLS = 1280
-EXTRA_SCALE_COLS = 320
+EXTRA_SCALE_COLS = 256
 HELD_AHEAD = 3
 DEFERRED = 3
 
@@ -47,7 +47,7 @@ def tile_modelnew_t_kernel(tc, x, weight, out):
         natural_pool = stack.enter_context(tc.tile_pool(name="natural", bufs=4))
         tree_pool = stack.enter_context(tc.tile_pool(name="tree", bufs=3))
         mx_pool = stack.enter_context(tc.tile_pool(name="mx", bufs=3))
-        result_pool = stack.enter_context(tc.tile_pool(name="result", bufs=3))
+        result_pool = stack.enter_context(tc.tile_pool(name="result", bufs=CHUNKS - 1))
         banks = stack.enter_context(tc.psum_pool(name="banks", bufs=8))
         stack.enter_context(tc.manual_schedule())
 
@@ -162,10 +162,8 @@ def tile_modelnew_t_kernel(tc, x, weight, out):
             clear_signs(magnitude[:, K + extra :], natural[:, extra:])
 
         def maximum_of(values, column):
-            unused = tree_pool.tile([P, CHUNK_COLS], BF16, name="unused")
-            width = values.shape[1]
             nc.vector.tensor_scalar(
-                out=unused[:, :width], in0=values, scalar1=0.0, scalar2=0.0, op0=ALU.max, op1=ALU.max, accum_out=column
+                out=values, in0=values, scalar1=0.0, scalar2=0.0, op0=ALU.max, op1=ALU.max, accum_out=column
             )
 
         def chunk_maximum(s):

@@ -28,7 +28,7 @@ WORDS = K // 2
 ABS_MASK = 0x7FFF7FFF
 FP8_MAX = 448.0
 EPS = 1e-12
-EXTRA_ABS_COLS = 64
+EXTRA_ABS_COLS = 128
 LATE_EXTRA_ABS_COLS = 1280
 EXTRA_SCALE_COLS = 256
 HELD_AHEAD = 3
@@ -130,7 +130,10 @@ def tile_modelnew_t_kernel(tc, x, weight, out):
             naturals[s] = natural
             first = s * CHUNK_COLS
             queue = nc.sync
-            queue.dma_start(out=chunk[:, :K], in_=x_flat[:, first : first + K])
+            held_width = K // 2 if s == 0 else K
+            for i in range(K // held_width):
+                cols = slice(i * held_width, (i + 1) * held_width)
+                queue.dma_start(out=chunk[:, cols], in_=x_flat[:, first + i * held_width : first + (i + 1) * held_width])
             pieces = FLOW_TILES if s == 0 else 1
             width = FLOW_COLS // pieces
             for i in range(pieces):
@@ -172,22 +175,26 @@ def tile_modelnew_t_kernel(tc, x, weight, out):
 
         load_and_transpose(0)
         first_magnitude = tree_pool.tile([P, CHUNK_COLS], BF16, name="magnitude")
-        first_sources = [grouped[0][:, :K]] + [naturals[0][:, i * K : (i + 1) * K] for i in range(FLOW_TILES)]
+        half = K // 2
 
-        def first_mask(i):
-            clear_signs(first_magnitude[:, i * K : (i + 1) * K], first_sources[i])
+        def first_mask(start, stop):
+            source = grouped[0] if stop <= K else naturals[0]
+            shift = 0 if stop <= K else K
+            clear_signs(first_magnitude[:, start:stop], source[:, start - shift : stop - shift])
 
-        def first_maximum(i):
-            maximum_of(first_magnitude[:, i * K : (i + 1) * K], maxima[:, i : i + 1])
+        def first_maximum(i, start, stop):
+            maximum_of(first_magnitude[:, start:stop], maxima[:, i : i + 1])
 
-        nc.scalar.activation(out=first_magnitude[:, K : 2 * K], in_=first_sources[1], func=ACT.Abs)
-        first_mask(0)
-        first_maximum(0)
-        first_mask(2)
-        first_maximum(1)
-        first_mask(3)
-        first_maximum(2)
-        first_maximum(3)
+        nc.scalar.activation(out=first_magnitude[:, half:K], in_=grouped[0][:, half:K], func=ACT.Abs)
+        nc.scalar.activation(out=first_magnitude[:, K : K + half], in_=naturals[0][:, :half], func=ACT.Abs)
+        first_mask(0, half)
+        first_maximum(0, 0, half)
+        first_mask(K + half, 2 * K)
+        first_mask(2 * K, 3 * K)
+        first_maximum(1, half, 2 * K)
+        first_mask(3 * K, 4 * K)
+        first_maximum(2, 2 * K, 3 * K)
+        first_maximum(3, 3 * K, 4 * K)
 
         w_facts = {}
         for s in range(1, CHUNKS):

from contextlib import ExitStack

import concourse.mybir as mybir
from concourse.masks import make_identity

F32 = mybir.dt.float32
BF16 = mybir.dt.bfloat16
I32 = mybir.dt.int32
U32 = mybir.dt.uint32
U8 = mybir.dt.uint8
FP8X4 = mybir.dt.float8_e4m3fn_x4
ALU = mybir.AluOpType
ACT = mybir.ActivationFunctionType
AX = mybir.AxisListType

P = 128
ROWS = 8192
K = 1024
N_OUT = 128
ROW_TILES = ROWS // P
TILES_PER_CHUNK = 4
CHUNKS = ROW_TILES // TILES_PER_CHUNK
CHUNK_COLS = TILES_PER_CHUNK * K
FLOW_TILES = TILES_PER_CHUNK - 1
FLOW_COLS = FLOW_TILES * K
PASSES = K // 512
WORDS = K // 2
ABS_MASK = 0x7FFF7FFF
FP8_MAX = 448.0
EPS = 1e-12
EXTRA_ABS_COLS = 128
LATE_EXTRA_ABS_COLS = 1280
EXTRA_SCALE_COLS = 256
HELD_AHEAD = 3
DEFERRED = 3

FLOPS = 2 * ROWS * K * N_OUT


def tile_modelnew_t_kernel(tc, x, weight, out):
    nc = tc.nc
    x_flat = x.flatten_outer_dims().rearrange("(p t) k -> p (t k)", t=ROW_TILES)
    out_flat = out.flatten_outer_dims().rearrange("(p t) n -> p (t n)", t=ROW_TILES)

    with ExitStack() as stack:
        keep = stack.enter_context(tc.tile_pool(name="keep", bufs=1))
        natural_pool = stack.enter_context(tc.tile_pool(name="natural", bufs=4))
        tree_pool = stack.enter_context(tc.tile_pool(name="tree", bufs=3))
        mx_pool = stack.enter_context(tc.tile_pool(name="mx", bufs=3))
        result_pool = stack.enter_context(tc.tile_pool(name="result", bufs=CHUNKS - 1))
        banks = stack.enter_context(tc.psum_pool(name="banks", bufs=8))
        stack.enter_context(tc.manual_schedule())

        identity = keep.tile([P, P], F32)
        make_identity(nc, identity[:])
        maxima = keep.tile([P, TILES_PER_CHUNK + CHUNKS - 1], F32)

        def column_of(columns, name):
            column = keep.tile([P, 1], F32, name=name + "_column")
            unused = keep.tile(columns.shape, F32, name=name + "_unused")
            nc.vector.tensor_scalar(
                out=unused[:],
                in0=columns,
                scalar1=1.0 / FP8_MAX,
                scalar2=EPS / FP8_MAX,
                op0=ALU.mult,
                op1=ALU.max,
                accum_out=column[:],
            )
            return column

        def turn(column, name):
            turned = banks.tile([P, P], F32, name=name + "_turned", tag="bank")
            nc.tensor.transpose(turned[:], column[:, 0:1].to_broadcast([P, P]), identity[:])
            return turned

        def inverse_scale_of(turned, name):
            inverse_scale = keep.tile([P, 1], F32, name=name + "_inverse_scale")
            nc.vector.reduce_max(out=inverse_scale[:], in_=turned[:], axis=AX.X)
            return inverse_scale

        def reciprocal_of(inverse_scale, name):
            the_scale = keep.tile([P, 1], F32, name=name + "_scale")
            nc.vector.reciprocal(out=the_scale[:], in_=inverse_scale[:])
            return the_scale

        def clear_signs(out_cols, in_cols):
            nc.vector.tensor_scalar(
                out=out_cols.bitcast(I32), in0=in_cols.bitcast(I32), scalar1=ABS_MASK, scalar2=None, op0=ALU.bitwise_and
            )

        def transpose_tile(words):
            flipped = banks.tile([P, WORDS], F32, name="flipped", tag="bank")
            for g in range(PASSES):
                for u in range(2):
                    a = 2 * g + u
                    nc.tensor.transpose(
                        flipped[:, a * P : (a + 1) * P], words[:, 256 * g + u : 256 * (g + 1) : 2], identity[:]
                    )
            return flipped

        w_raw = keep.tile([P, PASSES, 4 * N_OUT], BF16)
        w_flat = w_raw[:].rearrange("p g c -> p (g c)")
        w_abs = keep.tile([P, K], BF16)
        w_maximum = keep.tile([P, 1], F32)
        w_grouped = keep.tile([P, PASSES, N_OUT, 4], BF16, align_bytes=64)
        w_codes = keep.tile([P, PASSES * N_OUT], U32, align_bytes=64)
        w_scales = keep.tile([P, PASSES * N_OUT], U8, align_bytes=64)

        def weight_group(g, w_scale):
            nc.gpsimd.tensor_scalar(
                out=w_grouped[:, g],
                in0=w_raw[:, g, :].rearrange("p (j n) -> p n j", j=4),
                scalar1=w_scale[:, 0:1],
                scalar2=1.0,
                op0=ALU.mult,
                op1=ALU.mult,
            )

        grouped = []
        naturals = {}
        magnitudes = {}
        flow_banks = {}
        held_banks = {}

        def load_and_transpose(s):
            chunk = keep.tile([P, CHUNK_COLS], BF16, name="grouped%d" % s, align_bytes=64)
            grouped.append(chunk)
            natural = natural_pool.tile([P, FLOW_COLS], BF16, name="natural")
            naturals[s] = natural
            first = s * CHUNK_COLS
            queue = nc.sync
            held_width = K // 2 if s == 0 else K
            for i in range(K // held_width):
                cols = slice(i * held_width, (i + 1) * held_width)
                queue.dma_start(out=chunk[:, cols], in_=x_flat[:, first + i * held_width : first + (i + 1) * held_width])
            pieces = FLOW_TILES if s == 0 else 1
            width = FLOW_COLS // pieces
            for i in range(pieces):
                queue.dma_start(
                    out=natural[:, i * width : (i + 1) * width],
                    in_=x_flat[:, first + K + i * width : first + K + (i + 1) * width],
                )
            words = natural[:].bitcast(F32)
            for t in range(FLOW_TILES):
                flow_banks[(s, t)] = transpose_tile(words[:, t * WORDS : (t + 1) * WORDS])

        def copy_out(s):
            chunk_words = grouped[s][:].bitcast(F32).rearrange(
                "p (t g r u) -> p t g r u", t=TILES_PER_CHUNK, g=PASSES, r=P, u=2
            )
            for t in range(FLOW_TILES):
                nc.scalar.copy(
                    out=chunk_words[:, t + 1],
                    in_=flow_banks[(s, t)][:].rearrange("p (g u r) -> p g r u", g=PASSES, u=2, r=P),
                )

        def magnitude_of(s):
            natural = naturals[s]
            magnitude = tree_pool.tile([P, CHUNK_COLS], BF16, name="magnitude")
            magnitudes[s] = magnitude
            extra = LATE_EXTRA_ABS_COLS if s > CHUNKS - DEFERRED else EXTRA_ABS_COLS
            nc.scalar.activation(out=magnitude[:, :K], in_=grouped[s][:, :K], func=ACT.Abs)
            nc.scalar.activation(out=magnitude[:, K : K + extra], in_=natural[:, :extra], func=ACT.Abs)
            clear_signs(magnitude[:, K + extra :], natural[:, extra:])

        def maximum_of(values, column):
            nc.vector.tensor_scalar(
                out=values, in0=values, scalar1=0.0, scalar2=0.0, op0=ALU.max, op1=ALU.max, accum_out=column
            )

        def chunk_maximum(s):
            piece = TILES_PER_CHUNK - 1 + s
            maximum_of(magnitudes[s][:], maxima[:, piece : piece + 1])

        load_and_transpose(0)
        first_magnitude = tree_pool.tile([P, CHUNK_COLS], BF16, name="magnitude")
        half = K // 2

        def first_mask(start, stop):
            source = grouped[0] if stop <= K else naturals[0]
            shift = 0 if stop <= K else K
            clear_signs(first_magnitude[:, start:stop], source[:, start - shift : stop - shift])

        def first_maximum(i, start, stop):
            maximum_of(first_magnitude[:, start:stop], maxima[:, i : i + 1])

        nc.scalar.activation(out=first_magnitude[:, half:K], in_=grouped[0][:, half:K], func=ACT.Abs)
        nc.scalar.activation(out=first_magnitude[:, K : K + half], in_=naturals[0][:, :half], func=ACT.Abs)
        first_mask(0, half)
        first_maximum(0, 0, half)
        first_mask(K + half, 2 * K)
        first_mask(2 * K, 3 * K)
        first_maximum(1, half, 2 * K)
        first_mask(3 * K, 4 * K)
        first_maximum(2, 2 * K, 3 * K)
        first_maximum(3, 3 * K, 4 * K)

        w_facts = {}
        for s in range(1, CHUNKS):
            load_and_transpose(s)
            if s == 3:
                nc.sync.dma_start(out=w_raw[:], in_=weight.rearrange("(g p j) n -> p g (j n)", g=PASSES, p=P, j=4))
            if s == 2:
                chunk_maximum(1)
            magnitude_of(s)
            if s - 1 < CHUNKS - DEFERRED:
                copy_out(s - 1)
            if s >= 3:
                chunk_maximum(s - 1)
            if s == 5:
                nc.scalar.activation(out=w_abs[:], in_=w_flat, func=ACT.Abs)
            if s == 6:
                maximum_of(w_abs[:], w_maximum[:])
            if s == 7:
                w_facts["column"] = column_of(w_maximum[:], "w")
            if s == 10:
                w_facts["turned"] = turn(w_facts["column"], "w")
            if s == 11:
                w_facts["inverse_scale"] = inverse_scale_of(w_facts["turned"], "w")
            if s == 12:
                w_facts["scale"] = reciprocal_of(w_facts["inverse_scale"], "w")
                weight_group(0, w_facts["scale"])
                weight_group(1, w_facts["scale"])
        for s in range(CHUNKS - DEFERRED, CHUNKS):
            copy_out(s)

        def transpose_held(c):
            held_banks[c] = transpose_tile(grouped[c][:, :K].bitcast(F32))

        transpose_held(0)
        chunk_maximum(CHUNKS - 1)
        x_turned = turn(column_of(maxima[:], "x"), "x")
        for c in range(1, HELD_AHEAD):
            transpose_held(c)
        nc.vector.quantize_mx(
            out=w_codes[:].bitcast(FP8X4), scales=w_scales[:], in_=w_grouped[:].rearrange("p g n j -> p (g n j)")
        )
        x_inverse_scale = inverse_scale_of(x_turned, "x")
        x_scale = reciprocal_of(x_inverse_scale, "x")
        final_factor = keep.tile([P, 1], F32)
        nc.gpsimd.tensor_tensor(out=final_factor[:], in0=x_inverse_scale[:], in1=w_facts["inverse_scale"][:], op=ALU.mult)

        def scale(c):
            flat = grouped[c]
            pairs = held_banks[c][:].bitcast(BF16)
            for g in range(PASSES):
                cols = slice(g * 512, (g + 1) * 512)
                nc.scalar.activation(
                    out=flat[:, cols].rearrange("p (r u e) -> p r u e", r=P, u=2, e=2),
                    in_=pairs[:, cols].rearrange("p (u r e) -> p r u e", u=2, r=P, e=2),
                    func=ACT.Copy,
                    scale=x_scale[:, 0:1],
                )
            split = K + EXTRA_SCALE_COLS
            nc.scalar.activation(out=flat[:, K:split], in_=flat[:, K:split], func=ACT.Copy, scale=x_scale[:, 0:1])
            nc.vector.tensor_scalar(
                out=flat[:, split:], in0=flat[:, split:], scalar1=x_scale[:, 0:1], scalar2=None, op0=ALU.mult
            )

        def multiply(c, first_tile, tiles):
            width = tiles * K
            codes = mx_pool.tile([P, width // 4], U32, name="codes", align_bytes=64)
            scales = mx_pool.tile([P, width // 4], U8, name="scales", align_bytes=64)
            nc.vector.quantize_mx(
                out=codes[:].bitcast(FP8X4), scales=scales[:], in_=grouped[c][:, first_tile * K : first_tile * K + width]
            )
            acc = banks.tile([P, tiles, N_OUT], F32, name="acc", tag="bank")
            for t in range(tiles):
                for g in range(PASSES):
                    x_cols = slice((t * PASSES + g) * P, (t * PASSES + g + 1) * P)
                    w_cols = slice(g * N_OUT, (g + 1) * N_OUT)
                    nc.tensor.matmul_mx(
                        out=acc[:, t, :],
                        lhsT=codes[:, x_cols].bitcast(FP8X4),
                        lhsT_scale=scales[:, x_cols],
                        rhs=w_codes[:, w_cols].bitcast(FP8X4),
                        rhs_scale=w_scales[:, w_cols],
                        start=(g == 0),
                        stop=(g == PASSES - 1),
                    )
            return acc

        def finish(c, first_tile, tiles, acc):
            width = tiles * N_OUT
            if tiles == TILES_PER_CHUNK:
                result = result_pool.tile([P, width], F32, name="result")
            else:
                result = keep.tile([P, width], F32, name="piece%d" % first_tile)
            nc.scalar.activation(
                out=result[:], in_=acc[:].rearrange("p t n -> p (t n)"), func=ACT.Copy, scale=final_factor[:, 0:1]
            )
            first_col = (c * TILES_PER_CHUNK + first_tile) * N_OUT
            nc.sync.dma_start(out=out_flat[:, first_col : first_col + width], in_=result[:])

        scale(0)
        scale(1)
        products = {}
        for c in range(CHUNKS - 1):
            if c + HELD_AHEAD < CHUNKS:
                transpose_held(c + HELD_AHEAD)
            products[c] = multiply(c, 0, TILES_PER_CHUNK)
            if c + 2 < CHUNKS:
                scale(c + 2)
            if c >= 1:
                finish(c - 1, 0, TILES_PER_CHUNK, products[c - 1])
        last = CHUNKS - 1
        for t in range(TILES_PER_CHUNK):
            products[(last, t)] = multiply(last, t, 1)
            if t == 0:
                finish(last - 1, 0, TILES_PER_CHUNK, products[last - 1])
            else:
                finish(last, t - 1, 1, products[(last, t - 1)])
        finish(last, TILES_PER_CHUNK - 1, 1, products[(last, TILES_PER_CHUNK - 1)])
